import numpy as np
import ml_dtypes


def mxq(x, axis, fmt="e4m3"):
    dtype, down = {"e4m3": (ml_dtypes.float8_e4m3fn, 7), "e5m2": (ml_dtypes.float8_e5m2, 14)}[fmt]
    v = np.moveaxis(np.asarray(x, np.float32).astype(ml_dtypes.bfloat16).astype(np.float64), axis, -1)
    blocks = v.reshape(v.shape[:-1] + (-1, 32))
    amax = np.abs(blocks).max(-1, keepdims=True)
    byte = np.maximum(np.where(amax > 0, np.frexp(amax)[1] - 1 + 127, 0) - down, 1)
    scale = np.exp2(byte - 127.0)
    codes = (blocks / scale).astype(np.float32).astype(dtype).astype(np.float64)
    return np.moveaxis((codes * scale).reshape(v.shape), -1, axis)


WIDE = False


def mx_kscale(k):
    if not WIDE:
        return np.ones(k)
    levels = np.array([20, -20, 10, -10, 0])
    a = np.random.permutation(np.resize(levels, k // 512 * 4)).reshape(k // 512, 4)
    idx = np.arange(k)
    return np.exp2(a[idx // 512, idx % 128 // 32])


BF16 = ml_dtypes.bfloat16


def bf(x):
    return np.asarray(x, np.float32).astype(BF16)


def f64(x):
    return np.asarray(x).astype(np.float64)


B, IN, OUT = 1024, 2048, 2048
QI, QO = IN // 4, OUT // 4


def _hamilton_weight(Wr, Wi, Wj, Wk):
    return np.concatenate([
        np.concatenate([Wr, Wi, Wj, Wk], axis=1),
        np.concatenate([-Wi, Wr, Wk, -Wj], axis=1),
        np.concatenate([-Wj, -Wk, Wr, Wi], axis=1),
        np.concatenate([-Wk, Wj, -Wi, Wr], axis=1),
    ], axis=0)


def _hamilton_bias(br, bi, bj, bk):
    return np.concatenate([
        br - bi - bj - bk,
        br + bi + bj - bk,
        br - bi + bj + bk,
        br + bi - bj + bk,
    ], axis=0)


def _stack(a, q):
    return np.concatenate([a[:, c * q:(c + 1) * q] for c in range(4)], axis=0)


def setup_inputs():
    s = mx_kscale(B)[:, None]
    c = 1.0 / np.sqrt(QI)
    x = np.random.standard_normal((B, IN)) * s
    Wr = np.random.standard_normal((QI, QO)) * c
    Wi = np.random.standard_normal((QI, QO)) * c
    Wj = np.random.standard_normal((QI, QO)) * c
    Wk = np.random.standard_normal((QI, QO)) * c
    br = np.random.standard_normal(QO) * 0.3
    bi = np.random.standard_normal(QO) * 0.3
    bj = np.random.standard_normal(QO) * 0.3
    bk = np.random.standard_normal(QO) * 0.3
    g = np.random.standard_normal((B, OUT)) * np.exp2(np.random.randint(-12, 1, (B, 1))) / s
    return {"x": bf(x), "Wr": bf(Wr), "Wi": bf(Wi), "Wj": bf(Wj), "Wk": bf(Wk),
            "br": bf(br), "bi": bf(bi), "bj": bf(bj), "bk": bf(bk), "grad_out": bf(g)}


def reference(x, Wr, Wi, Wj, Wk, br, bi, bj, bk, grad_out):
    xq = mxq(f64(x), 0, "e4m3")
    gq = mxq(f64(grad_out), 0, "e5m2")
    return _stack(xq, QI).T @ _stack(gq, QO)

@@ -1,0 +1,122 @@
+from contextlib import ExitStack
+
+import concourse.mybir as mybir
+
+BF16 = mybir.dt.bfloat16
+F32 = mybir.dt.float32
+U32 = mybir.dt.uint32
+U8 = mybir.dt.uint8
+E4M3_X4 = mybir.dt.float8_e4m3fn_x4
+E5M2_X4 = mybir.dt.float8_e5m2_x4
+
+P = 128
+PACK = 4
+K_PASS = P * PACK
+TOKENS = 1024
+CHUNK = 512
+CHUNKS = 4
+TOKEN_HALVES = TOKENS // K_PASS
+PASSES = TOKEN_HALVES * CHUNKS
+M_TILES = CHUNK // P
+LOAD_CHUNKS = 2
+LOAD_COLS = LOAD_CHUNKS * CHUNK
+VECTOR_COLS = CHUNK // 2
+RUN = 4
+
+FLOPS = 2 * CHUNK * CHUNK * CHUNKS * TOKENS
+BYTES = 2 * TOKENS * CHUNKS * CHUNK * 2 + CHUNK * CHUNK * 4
+
+
+def tile_quaternionlinear_kernel(tc, x, Wr, Wi, Wj, Wk, br, bi, bj, bk, grad_out, out):
+    nc = tc.nc
+    sources = {"x": x, "g": grad_out}
+    formats = {"x": E4M3_X4, "g": E5M2_X4}
+
+    with ExitStack() as ctx:
+        raw_pool = ctx.enter_context(tc.tile_pool(name="raw", bufs=1))
+        grouped_pool = ctx.enter_context(tc.tile_pool(name="grouped", bufs=1))
+        keep = ctx.enter_context(tc.tile_pool(name="keep", bufs=1))
+        result_pool = ctx.enter_context(tc.tile_pool(name="result", bufs=1))
+        psum = ctx.enter_context(tc.psum_pool(name="psum", bufs=1))
+        ctx.enter_context(tc.manual_schedule())
+
+        codes = {}
+        scales = {}
+        for name in ("x", "g"):
+            codes[name] = keep.tile([P, PASSES, CHUNK], U32, name="codes_" + name, align_bytes=64)
+            scales[name] = keep.tile([P, PASSES, CHUNK], U8, name="scales_" + name, align_bytes=64)
+        acc = [psum.tile([P, CHUNK], F32, name="acc_%d" % m) for m in range(M_TILES)]
+
+        raw = {}
+        units = []
+        for half in range(TOKEN_HALVES):
+            token_rows = slice(half * K_PASS, (half + 1) * K_PASS)
+            for first_chunk in range(0, CHUNKS, LOAD_CHUNKS):
+                cols = slice(first_chunk * CHUNK, first_chunk * CHUNK + LOAD_COLS)
+                for name in ("x", "g"):
+                    piece = raw_pool.tile(
+                        [P, PACK, LOAD_COLS], BF16, name="raw_%s_%d_%d" % (name, half, first_chunk)
+                    )
+                    nc.sync.dma_start(
+                        out=piece[:],
+                        in_=sources[name][token_rows, cols].rearrange("(p j) w -> p j w", j=PACK),
+                    )
+                    for chunk in range(first_chunk, first_chunk + LOAD_CHUNKS):
+                        chunk_cols = slice((chunk - first_chunk) * CHUNK, (chunk - first_chunk + 1) * CHUNK)
+                        raw[(name, half, chunk)] = piece[:, :, chunk_cols]
+                        units.append((name, half, chunk))
+
+        grouped = {}
+
+        def regroup(unit):
+            tile = grouped_pool.tile([P, CHUNK, PACK], BF16, name="grouped_%s_%d_%d" % unit, align_bytes=64)
+            grouped[unit] = tile
+            vector_cols = slice(0, VECTOR_COLS)
+            scalar_cols = slice(VECTOR_COLS, CHUNK)
+            nc.vector.tensor_copy(
+                out=tile[:, vector_cols, :].rearrange("p (c i) j -> p c j i", i=RUN),
+                in_=raw[unit][:, :, vector_cols].rearrange("p j (c i) -> p c j i", i=RUN),
+            )
+            nc.scalar.copy(
+                out=tile[:, scalar_cols, :].rearrange("p (c i) j -> p c j i", i=RUN),
+                in_=raw[unit][:, :, scalar_cols].rearrange("p j (c i) -> p c j i", i=RUN),
+            )
+
+        def quantise(unit):
+            name, half, chunk = unit
+            k = half * CHUNKS + chunk
+            nc.vector.quantize_mx(
+                out=codes[name][:, k, :].bitcast(formats[name]),
+                scales=scales[name][:, k, :],
+                in_=grouped[unit][:].rearrange("p w j -> p (w j)"),
+            )
+
+        def multiply(k):
+            for m in range(M_TILES):
+                m_cols = slice(m * P, (m + 1) * P)
+                nc.tensor.matmul_mx(
+                    out=acc[m][:],
+                    lhsT=codes["x"][:, k, m_cols].bitcast(E4M3_X4),
+                    lhsT_scale=scales["x"][:, k, m_cols],
+                    rhs=codes["g"][:, k, :].bitcast(E5M2_X4),
+                    rhs_scale=scales["g"][:, k, :],
+                    start=(k == 0),
+                    stop=(k == PASSES - 1),
+                )
+
+        for step in range(len(units) + 1):
+            if step < len(units):
+                regroup(units[step])
+            if step >= 1:
+                name, half, chunk = units[step - 1]
+                quantise(units[step - 1])
+                if name == "g":
+                    multiply(half * CHUNKS + chunk)
+
+        for m in range(M_TILES):
+            result = result_pool.tile([P, CHUNK], F32, name="result_%d" % m)
+            if m % 2 == 0:
+                nc.scalar.copy(out=result[:], in_=acc[m][:])
+            else:
+                nc.vector.tensor_copy(out=result[:], in_=acc[m][:])
+            nc.sync.dma_start(out=out[m * P : (m + 1) * P, :], in_=result[:])

@@ -13,18 +13,16 @@ P = 128
 PACK = 4
 K_PASS = P * PACK
 TOKENS = 1024
+TOKEN_HALVES = TOKENS // K_PASS
 CHUNK = 512
 CHUNKS = 4
-TOKEN_HALVES = TOKENS // K_PASS
-PASSES = TOKEN_HALVES * CHUNKS
+COLS = CHUNKS * CHUNK
 M_TILES = CHUNK // P
-LOAD_CHUNKS = 2
-LOAD_COLS = LOAD_CHUNKS * CHUNK
-VECTOR_COLS = CHUNK // 2
+LOAD_COLS = 2 * CHUNK
 RUN = 4
 
 FLOPS = 2 * CHUNK * CHUNK * CHUNKS * TOKENS
-BYTES = 2 * TOKENS * CHUNKS * CHUNK * 2 + CHUNK * CHUNK * 4
+BYTES = 2 * TOKENS * COLS * 2 + CHUNK * CHUNK * 4
 
 
 def tile_quaternionlinear_kernel(tc, x, Wr, Wi, Wj, Wk, br, bi, bj, bk, grad_out, out):
@@ -43,36 +41,39 @@ def tile_quaternionlinear_kernel(tc, x, Wr, Wi, Wj, Wk, br, bi, bj, bk, grad_out
         codes = {}
         scales = {}
         for name in ("x", "g"):
-            codes[name] = keep.tile([P, PASSES, CHUNK], U32, name="codes_" + name, align_bytes=64)
-            scales[name] = keep.tile([P, PASSES, CHUNK], U8, name="scales_" + name, align_bytes=64)
+            codes[name] = keep.tile([P, TOKEN_HALVES, COLS], U32, name="codes_" + name, align_bytes=64)
+            scales[name] = keep.tile([P, TOKEN_HALVES, COLS], U8, name="scales_" + name, align_bytes=64)
         acc = [psum.tile([P, CHUNK], F32, name="acc_%d" % m) for m in range(M_TILES)]
 
         raw = {}
         units = []
         for half in range(TOKEN_HALVES):
             token_rows = slice(half * K_PASS, (half + 1) * K_PASS)
-            for first_chunk in range(0, CHUNKS, LOAD_CHUNKS):
-                cols = slice(first_chunk * CHUNK, first_chunk * CHUNK + LOAD_COLS)
-                for name in ("x", "g"):
-                    piece = raw_pool.tile(
-                        [P, PACK, LOAD_COLS], BF16, name="raw_%s_%d_%d" % (name, half, first_chunk)
-                    )
+            for load_col in range(0, COLS, LOAD_COLS):
+                for name in ("g", "x"):
+                    piece = raw_pool.tile([P, PACK, LOAD_COLS], BF16, name="raw_%s_%d_%d" % (name, half, load_col))
                     nc.sync.dma_start(
                         out=piece[:],
-                        in_=sources[name][token_rows, cols].rearrange("(p j) w -> p j w", j=PACK),
+                        in_=sources[name][token_rows, load_col : load_col + LOAD_COLS].rearrange(
+                            "(p j) w -> p j w", j=PACK
+                        ),
                     )
-                    for chunk in range(first_chunk, first_chunk + LOAD_CHUNKS):
-                        chunk_cols = slice((chunk - first_chunk) * CHUNK, (chunk - first_chunk + 1) * CHUNK)
-                        raw[(name, half, chunk)] = piece[:, :, chunk_cols]
-                        units.append((name, half, chunk))
+                    for chunk_col in range(load_col, load_col + LOAD_COLS, CHUNK):
+                        is_last = name == "x" and half == TOKEN_HALVES - 1 and chunk_col == COLS - CHUNK
+                        width = P if is_last else CHUNK
+                        for col in range(chunk_col, chunk_col + CHUNK, width):
+                            unit = (name, half, col, width)
+                            raw[unit] = piece[:, :, col - load_col : col - load_col + width]
+                            units.append(unit)
 
         grouped = {}
 
         def regroup(unit):
-            tile = grouped_pool.tile([P, CHUNK, PACK], BF16, name="grouped_%s_%d_%d" % unit, align_bytes=64)
+            width = unit[3]
+            tile = grouped_pool.tile([P, width, PACK], BF16, name="grouped_%s_%d_%d_%d" % unit, align_bytes=64)
             grouped[unit] = tile
-            vector_cols = slice(0, VECTOR_COLS)
-            scalar_cols = slice(VECTOR_COLS, CHUNK)
+            vector_cols = slice(0, width // 2)
+            scalar_cols = slice(width // 2, width)
             nc.vector.tensor_copy(
                 out=tile[:, vector_cols, :].rearrange("p (c i) j -> p c j i", i=RUN),
                 in_=raw[unit][:, :, vector_cols].rearrange("p j (c i) -> p c j i", i=RUN),
@@ -83,35 +84,35 @@ def tile_quaternionlinear_kernel(tc, x, Wr, Wi, Wj, Wk, br, bi, bj, bk, grad_out
             )
 
         def quantise(unit):
-            name, half, chunk = unit
-            k = half * CHUNKS + chunk
+            name, half, col, width = unit
             nc.vector.quantize_mx(
-                out=codes[name][:, k, :].bitcast(formats[name]),
-                scales=scales[name][:, k, :],
+                out=codes[name][:, half, col : col + width].bitcast(formats[name]),
+                scales=scales[name][:, half, col : col + width],
                 in_=grouped[unit][:].rearrange("p w j -> p (w j)"),
             )
 
-        def multiply(k):
-            for m in range(M_TILES):
-                m_cols = slice(m * P, (m + 1) * P)
+        def multiply(unit):
+            name, half, col, width = unit
+            for m_col in range(col, col + width, P):
+                chunk = m_col // CHUNK
+                chunk_cols = slice(chunk * CHUNK, (chunk + 1) * CHUNK)
                 nc.tensor.matmul_mx(
-                    out=acc[m][:],
-                    lhsT=codes["x"][:, k, m_cols].bitcast(E4M3_X4),
-                    lhsT_scale=scales["x"][:, k, m_cols],
-                    rhs=codes["g"][:, k, :].bitcast(E5M2_X4),
-                    rhs_scale=scales["g"][:, k, :],
-                    start=(k == 0),
-                    stop=(k == PASSES - 1),
+                    out=acc[(m_col % CHUNK) // P][:],
+                    lhsT=codes["x"][:, half, m_col : m_col + P].bitcast(E4M3_X4),
+                    lhsT_scale=scales["x"][:, half, m_col : m_col + P],
+                    rhs=codes["g"][:, half, chunk_cols].bitcast(E5M2_X4),
+                    rhs_scale=scales["g"][:, half, chunk_cols],
+                    start=(half == 0 and chunk == 0),
+                    stop=(half == TOKEN_HALVES - 1 and chunk == CHUNKS - 1),
                 )
 
         for step in range(len(units) + 1):
             if step < len(units):
                 regroup(units[step])
             if step >= 1:
-                name, half, chunk = units[step - 1]
                 quantise(units[step - 1])
-                if name == "g":
-                    multiply(half * CHUNKS + chunk)
+                if units[step - 1][0] == "x":
+                    multiply(units[step - 1])
 
         for m in range(M_TILES):
             result = result_pool.tile([P, CHUNK], F32, name="result_%d" % m)

@@ -19,6 +19,8 @@ CHUNKS = 4
 COLS = CHUNKS * CHUNK
 M_TILES = CHUNK // P
 LOAD_COLS = 2 * CHUNK
+TAIL_COLS = 2 * P
+STORE_COLS = CHUNK // 2
 RUN = 4
 
 FLOPS = 2 * CHUNK * CHUNK * CHUNKS * TOKENS
@@ -59,8 +61,8 @@ def tile_quaternionlinear_kernel(tc, x, Wr, Wi, Wj, Wk, br, bi, bj, bk, grad_out
                         ),
                     )
                     for chunk_col in range(load_col, load_col + LOAD_COLS, CHUNK):
-                        is_last = name == "x" and half == TOKEN_HALVES - 1 and chunk_col == COLS - CHUNK
-                        width = P if is_last else CHUNK
+                        is_last = name == "x" and half == TOKEN_HALVES - 1 and load_col == COLS - LOAD_COLS
+                        width = TAIL_COLS if is_last else CHUNK
                         for col in range(chunk_col, chunk_col + CHUNK, width):
                             unit = (name, half, col, width)
                             raw[unit] = piece[:, :, col - load_col : col - load_col + width]
@@ -115,9 +117,10 @@ def tile_quaternionlinear_kernel(tc, x, Wr, Wi, Wj, Wk, br, bi, bj, bk, grad_out
                     multiply(units[step - 1])
 
         for m in range(M_TILES):
-            result = result_pool.tile([P, CHUNK], F32, name="result_%d" % m)
-            if m % 2 == 0:
-                nc.scalar.copy(out=result[:], in_=acc[m][:])
-            else:
-                nc.vector.tensor_copy(out=result[:], in_=acc[m][:])
-            nc.sync.dma_start(out=out[m * P : (m + 1) * P, :], in_=result[:])
+            for col in range(0, CHUNK, STORE_COLS):
+                result = result_pool.tile([P, STORE_COLS], F32, name="result_%d_%d" % (m, col))
+                if m % 2 == 0:
+                    nc.scalar.copy(out=result[:], in_=acc[m][:, col : col + STORE_COLS])
+                else:
+                    nc.vector.tensor_copy(out=result[:], in_=acc[m][:, col : col + STORE_COLS])
+                nc.sync.dma_start(out=out[m * P : (m + 1) * P, col : col + STORE_COLS], in_=result[:])

@@ -45,6 +45,8 @@ def tile_quaternionlinear_kernel(tc, x, Wr, Wi, Wj, Wk, br, bi, bj, bk, grad_out
         for name in ("x", "g"):
             codes[name] = keep.tile([P, TOKEN_HALVES, COLS], U32, name="codes_" + name, align_bytes=64)
             scales[name] = keep.tile([P, TOKEN_HALVES, COLS], U8, name="scales_" + name, align_bytes=64)
+        tail_codes = keep.tile([P, M_TILES, TAIL_COLS], U32, name="tail_codes", align_bytes=64)
+        tail_scales = keep.tile([P, M_TILES, TAIL_COLS], U8, name="tail_scales", align_bytes=64)
         acc = [psum.tile([P, CHUNK], F32, name="acc_%d" % m) for m in range(M_TILES)]
 
         raw = {}
@@ -60,12 +62,16 @@ def tile_quaternionlinear_kernel(tc, x, Wr, Wi, Wj, Wk, br, bi, bj, bk, grad_out
                             "(p j) w -> p j w", j=PACK
                         ),
                     )
-                    for chunk_col in range(load_col, load_col + LOAD_COLS, CHUNK):
-                        is_last = name == "x" and half == TOKEN_HALVES - 1 and load_col == COLS - LOAD_COLS
-                        width = TAIL_COLS if is_last else CHUNK
-                        for col in range(chunk_col, chunk_col + CHUNK, width):
-                            unit = (name, half, col, width)
-                            raw[unit] = piece[:, :, col - load_col : col - load_col + width]
+                    if name == "x" and half == TOKEN_HALVES - 1 and load_col == COLS - LOAD_COLS:
+                        for m in range(M_TILES):
+                            unit = ("tail", half, m, TAIL_COLS)
+                            raw[unit] = [piece[:, :, k * CHUNK + m * P : k * CHUNK + (m + 1) * P] for k in range(2)]
+                            units.append(unit)
+                    else:
+                        for col in range(load_col, load_col + LOAD_COLS, CHUNK):
+                            unit = (name, half, col, CHUNK)
+                            first = col - load_col
+                            raw[unit] = [piece[:, :, first + k * (CHUNK // 2) : first + (k + 1) * (CHUNK // 2)] for k in range(2)]
                             units.append(unit)
 
         grouped = {}
@@ -74,34 +80,43 @@ def tile_quaternionlinear_kernel(tc, x, Wr, Wi, Wj, Wk, br, bi, bj, bk, grad_out
             width = unit[3]
             tile = grouped_pool.tile([P, width, PACK], BF16, name="grouped_%s_%d_%d_%d" % unit, align_bytes=64)
             grouped[unit] = tile
-            vector_cols = slice(0, width // 2)
-            scalar_cols = slice(width // 2, width)
             nc.vector.tensor_copy(
-                out=tile[:, vector_cols, :].rearrange("p (c i) j -> p c j i", i=RUN),
-                in_=raw[unit][:, :, vector_cols].rearrange("p j (c i) -> p c j i", i=RUN),
+                out=tile[:, : width // 2, :].rearrange("p (c i) j -> p c j i", i=RUN),
+                in_=raw[unit][0].rearrange("p j (c i) -> p c j i", i=RUN),
             )
             nc.scalar.copy(
-                out=tile[:, scalar_cols, :].rearrange("p (c i) j -> p c j i", i=RUN),
-                in_=raw[unit][:, :, scalar_cols].rearrange("p j (c i) -> p c j i", i=RUN),
+                out=tile[:, width // 2 :, :].rearrange("p (c i) j -> p c j i", i=RUN),
+                in_=raw[unit][1].rearrange("p j (c i) -> p c j i", i=RUN),
             )
 
         def quantise(unit):
             name, half, col, width = unit
-            nc.vector.quantize_mx(
-                out=codes[name][:, half, col : col + width].bitcast(formats[name]),
-                scales=scales[name][:, half, col : col + width],
-                in_=grouped[unit][:].rearrange("p w j -> p (w j)"),
-            )
+            if name == "tail":
+                codes_out = tail_codes[:, col, :].bitcast(E4M3_X4)
+                scales_out = tail_scales[:, col, :]
+            else:
+                codes_out = codes[name][:, half, col : col + width].bitcast(formats[name])
+                scales_out = scales[name][:, half, col : col + width]
+            nc.vector.quantize_mx(out=codes_out, scales=scales_out, in_=grouped[unit][:].rearrange("p w j -> p (w j)"))
 
         def multiply(unit):
             name, half, col, width = unit
-            for m_col in range(col, col + width, P):
-                chunk = m_col // CHUNK
+            for k in range(width // P):
+                if name == "tail":
+                    m = col
+                    chunk = CHUNKS - 2 + k
+                    x_codes = tail_codes[:, m, k * P : (k + 1) * P]
+                    x_scales = tail_scales[:, m, k * P : (k + 1) * P]
+                else:
+                    m = k
+                    chunk = col // CHUNK
+                    x_codes = codes["x"][:, half, col + k * P : col + (k + 1) * P]
+                    x_scales = scales["x"][:, half, col + k * P : col + (k + 1) * P]
                 chunk_cols = slice(chunk * CHUNK, (chunk + 1) * CHUNK)
                 nc.tensor.matmul_mx(
-                    out=acc[(m_col % CHUNK) // P][:],
-                    lhsT=codes["x"][:, half, m_col : m_col + P].bitcast(E4M3_X4),
-                    lhsT_scale=scales["x"][:, half, m_col : m_col + P],
+                    out=acc[m][:],
+                    lhsT=x_codes.bitcast(E4M3_X4),
+                    lhsT_scale=x_scales,
                     rhs=codes["g"][:, half, chunk_cols].bitcast(E5M2_X4),
                     rhs_scale=scales["g"][:, half, chunk_cols],
                     start=(half == 0 and chunk == 0),
@@ -113,13 +128,13 @@ def tile_quaternionlinear_kernel(tc, x, Wr, Wi, Wj, Wk, br, bi, bj, bk, grad_out
                 regroup(units[step])
             if step >= 1:
                 quantise(units[step - 1])
-                if units[step - 1][0] == "x":
+                if units[step - 1][0] != "g":
                     multiply(units[step - 1])
 
         for m in range(M_TILES):
             for col in range(0, CHUNK, STORE_COLS):
                 result = result_pool.tile([P, STORE_COLS], F32, name="result_%d_%d" % (m, col))
-                if m % 2 == 0:
+                if m < M_TILES - 1:
                     nc.scalar.copy(out=result[:], in_=acc[m][:, col : col + STORE_COLS])
                 else:
                     nc.vector.tensor_copy(out=result[:], in_=acc[m][:, col : col + STORE_COLS])

@@ -19,7 +19,10 @@ CHUNKS = 4
 COLS = CHUNKS * CHUNK
 M_TILES = CHUNK // P
 LOAD_COLS = 2 * CHUNK
-TAIL_COLS = 2 * P
+TAIL_COLS = P
+TAIL_UNITS = LOAD_COLS // TAIL_COLS
+TAIL_VECTOR = 64
+TAIL_LOAD = 6 * P
 STORE_COLS = CHUNK // 2
 RUN = 4
 
@@ -45,8 +48,8 @@ def tile_quaternionlinear_kernel(tc, x, Wr, Wi, Wj, Wk, br, bi, bj, bk, grad_out
         for name in ("x", "g"):
             codes[name] = keep.tile([P, TOKEN_HALVES, COLS], U32, name="codes_" + name, align_bytes=64)
             scales[name] = keep.tile([P, TOKEN_HALVES, COLS], U8, name="scales_" + name, align_bytes=64)
-        tail_codes = keep.tile([P, M_TILES, TAIL_COLS], U32, name="tail_codes", align_bytes=64)
-        tail_scales = keep.tile([P, M_TILES, TAIL_COLS], U8, name="tail_scales", align_bytes=64)
+        tail_codes = keep.tile([P, TAIL_UNITS, TAIL_COLS], U32, name="tail_codes", align_bytes=64)
+        tail_scales = keep.tile([P, TAIL_UNITS, TAIL_COLS], U8, name="tail_scales", align_bytes=64)
         acc = [psum.tile([P, CHUNK], F32, name="acc_%d" % m) for m in range(M_TILES)]
 
         raw = {}
@@ -56,22 +59,28 @@ def tile_quaternionlinear_kernel(tc, x, Wr, Wi, Wj, Wk, br, bi, bj, bk, grad_out
             for load_col in range(0, COLS, LOAD_COLS):
                 for name in ("g", "x"):
                     piece = raw_pool.tile([P, PACK, LOAD_COLS], BF16, name="raw_%s_%d_%d" % (name, half, load_col))
-                    nc.sync.dma_start(
-                        out=piece[:],
-                        in_=sources[name][token_rows, load_col : load_col + LOAD_COLS].rearrange(
-                            "(p j) w -> p j w", j=PACK
-                        ),
-                    )
-                    if name == "x" and half == TOKEN_HALVES - 1 and load_col == COLS - LOAD_COLS:
-                        for m in range(M_TILES):
-                            unit = ("tail", half, m, TAIL_COLS)
-                            raw[unit] = [piece[:, :, k * CHUNK + m * P : k * CHUNK + (m + 1) * P] for k in range(2)]
+                    last = name == "x" and half == TOKEN_HALVES - 1 and load_col == COLS - LOAD_COLS
+                    cuts = [0, TAIL_LOAD, LOAD_COLS] if last else [0, LOAD_COLS]
+                    for begin, end in zip(cuts, cuts[1:]):
+                        nc.sync.dma_start(
+                            out=piece[:, :, begin:end],
+                            in_=sources[name][token_rows, load_col + begin : load_col + end].rearrange(
+                                "(p j) w -> p j w", j=PACK
+                            ),
+                        )
+                    if last:
+                        for n in range(TAIL_UNITS):
+                            m, k = divmod(n, 2)
+                            unit = ("tail", half, n, TAIL_COLS)
+                            first = k * CHUNK + m * P
+                            raw[unit] = [piece[:, :, first : first + TAIL_VECTOR], piece[:, :, first + TAIL_VECTOR : first + TAIL_COLS]]
                             units.append(unit)
                     else:
                         for col in range(load_col, load_col + LOAD_COLS, CHUNK):
                             unit = (name, half, col, CHUNK)
                             first = col - load_col
-                            raw[unit] = [piece[:, :, first + k * (CHUNK // 2) : first + (k + 1) * (CHUNK // 2)] for k in range(2)]
+                            raw[unit] = [piece[:, :, first : first + CHUNK] if col == load_col else None,
+                                         piece[:, :, first : first + CHUNK] if col != load_col else None]
                             units.append(unit)
 
         grouped = {}
@@ -80,14 +89,17 @@ def tile_quaternionlinear_kernel(tc, x, Wr, Wi, Wj, Wk, br, bi, bj, bk, grad_out
             width = unit[3]
             tile = grouped_pool.tile([P, width, PACK], BF16, name="grouped_%s_%d_%d_%d" % unit, align_bytes=64)
             grouped[unit] = tile
-            nc.vector.tensor_copy(
-                out=tile[:, : width // 2, :].rearrange("p (c i) j -> p c j i", i=RUN),
-                in_=raw[unit][0].rearrange("p j (c i) -> p c j i", i=RUN),
-            )
-            nc.scalar.copy(
-                out=tile[:, width // 2 :, :].rearrange("p (c i) j -> p c j i", i=RUN),
-                in_=raw[unit][1].rearrange("p j (c i) -> p c j i", i=RUN),
-            )
+            whole = unit[0] != "tail"
+            if raw[unit][0] is not None:
+                nc.vector.tensor_copy(
+                    out=tile[:, : width if whole else TAIL_VECTOR, :].rearrange("p (c i) j -> p c j i", i=RUN),
+                    in_=raw[unit][0].rearrange("p j (c i) -> p c j i", i=RUN),
+                )
+            if raw[unit][1] is not None:
+                nc.scalar.copy(
+                    out=tile[:, 0 if whole else TAIL_VECTOR :, :].rearrange("p (c i) j -> p c j i", i=RUN),
+                    in_=raw[unit][1].rearrange("p j (c i) -> p c j i", i=RUN),
+                )
 
         def quantise(unit):
             name, half, col, width = unit
@@ -103,10 +115,10 @@ def tile_quaternionlinear_kernel(tc, x, Wr, Wi, Wj, Wk, br, bi, bj, bk, grad_out
             name, half, col, width = unit
             for k in range(width // P):
                 if name == "tail":
-                    m = col
-                    chunk = CHUNKS - 2 + k
-                    x_codes = tail_codes[:, m, k * P : (k + 1) * P]
-                    x_scales = tail_scales[:, m, k * P : (k + 1) * P]
+                    m = col // 2
+                    chunk = CHUNKS - 2 + col % 2
+                    x_codes = tail_codes[:, col, :]
+                    x_scales = tail_scales[:, col, :]
                 else:
                     m = k
                     chunk = col // CHUNK
@@ -123,13 +135,27 @@ def tile_quaternionlinear_kernel(tc, x, Wr, Wi, Wj, Wk, br, bi, bj, bk, grad_out
                     stop=(half == TOKEN_HALVES - 1 and chunk == CHUNKS - 1),
                 )
 
-        for step in range(len(units) + 1):
-            if step < len(units):
-                regroup(units[step])
-            if step >= 1:
-                quantise(units[step - 1])
-                if units[step - 1][0] != "g":
-                    multiply(units[step - 1])
+        def finish(unit):
+            quantise(unit)
+            if unit[0] != "g":
+                multiply(unit)
+
+        waiting = []
+        for i, unit in enumerate(units):
+            regroup(unit)
+            if unit[0] == "tail" or i % 2 == 1:
+                if unit[0] == "tail":
+                    finish(waiting.pop(0))
+                    waiting.append(unit)
+                else:
+                    if len(waiting) == 2:
+                        finish(waiting.pop(0))
+                    finish(waiting.pop(0))
+                    waiting.append(unit)
+            else:
+                waiting.append(unit)
+        for unit in waiting:
+            finish(unit)
 
         for m in range(M_TILES):
             for col in range(0, CHUNK, STORE_COLS):

@@ -21,7 +21,7 @@ M_TILES = CHUNK // P
 LOAD_COLS = 2 * CHUNK
 TAIL_COLS = P
 TAIL_UNITS = LOAD_COLS // TAIL_COLS
-TAIL_VECTOR = 64
+TAIL_VECTOR = 48
 TAIL_LOAD = 6 * P
 STORE_COLS = CHUNK // 2
 RUN = 4

@@ -1,6 +1,7 @@
 from contextlib import ExitStack
 
 import concourse.mybir as mybir
+from concourse.masks import make_identity
 
 BF16 = mybir.dt.bfloat16
 F32 = mybir.dt.float32
@@ -24,6 +25,8 @@ TAIL_UNITS = LOAD_COLS // TAIL_COLS
 TAIL_VECTOR = 48
 TAIL_LOAD = 6 * P
 STORE_COLS = CHUNK // 2
+PE_COLS = P
+PE_BANKS = 4
 RUN = 4
 
 FLOPS = 2 * CHUNK * CHUNK * CHUNKS * TOKENS
@@ -50,6 +53,8 @@ def tile_quaternionlinear_kernel(tc, x, Wr, Wi, Wj, Wk, br, bi, bj, bk, grad_out
             scales[name] = keep.tile([P, TOKEN_HALVES, COLS], U8, name="scales_" + name, align_bytes=64)
         tail_codes = keep.tile([P, TAIL_UNITS, TAIL_COLS], U32, name="tail_codes", align_bytes=64)
         tail_scales = keep.tile([P, TAIL_UNITS, TAIL_COLS], U8, name="tail_scales", align_bytes=64)
+        identity = keep.tile([P, P], BF16, name="identity")
+        make_identity(nc, identity[:])
         acc = [psum.tile([P, CHUNK], F32, name="acc_%d" % m) for m in range(M_TILES)]
 
         raw = {}
@@ -85,6 +90,20 @@ def tile_quaternionlinear_kernel(tc, x, Wr, Wi, Wj, Wk, br, bi, bj, bk, grad_out
 
         grouped = {}
 
+        passes = {}
+
+        def tensor_pass(unit):
+            n = len(passes)
+            bank = psum.tile([P, PE_COLS, PACK], BF16, name="bank_%d" % (n % PE_BANKS))
+            passes[unit] = bank
+            nc.tensor.matmul(
+                out=bank[:].rearrange("p c j -> p (c j)"),
+                lhsT=identity[:],
+                rhs=raw[unit][1][:, :, CHUNK - PE_COLS :].rearrange("p j c -> p c j"),
+                start=True,
+                stop=True,
+            )
+
         def regroup(unit):
             width = unit[3]
             tile = grouped_pool.tile([P, width, PACK], BF16, name="grouped_%s_%d_%d_%d" % unit, align_bytes=64)
@@ -96,10 +115,14 @@ def tile_quaternionlinear_kernel(tc, x, Wr, Wi, Wj, Wk, br, bi, bj, bk, grad_out
                     in_=raw[unit][0].rearrange("p j (c i) -> p c j i", i=RUN),
                 )
             if raw[unit][1] is not None:
+                begin = 0 if whole else TAIL_VECTOR
+                end = width - PE_COLS if unit in passes else width
                 nc.scalar.copy(
-                    out=tile[:, 0 if whole else TAIL_VECTOR :, :].rearrange("p (c i) j -> p c j i", i=RUN),
-                    in_=raw[unit][1].rearrange("p j (c i) -> p c j i", i=RUN),
+                    out=tile[:, begin:end, :].rearrange("p (c i) j -> p c j i", i=RUN),
+                    in_=raw[unit][1][:, :, : end - begin].rearrange("p j (c i) -> p c j i", i=RUN),
                 )
+                if unit in passes:
+                    nc.scalar.copy(out=tile[:, end:, :], in_=passes[unit][:])
 
         def quantise(unit):
             name, half, col, width = unit
@@ -143,6 +166,8 @@ def tile_quaternionlinear_kernel(tc, x, Wr, Wi, Wj, Wk, br, bi, bj, bk, grad_out
         waiting = []
         for i, unit in enumerate(units):
             regroup(unit)
+            if i % 2 == 1 and i + 2 < len(units) - TAIL_UNITS:
+                tensor_pass(units[i + 2])
             if unit[0] == "tail" or i % 2 == 1:
                 if unit[0] == "tail":
                     finish(waiting.pop(0))

@@ -97,9 +97,9 @@ def tile_quaternionlinear_kernel(tc, x, Wr, Wi, Wj, Wk, br, bi, bj, bk, grad_out
             bank = psum.tile([P, PE_COLS, PACK], BF16, name="bank_%d" % (n % PE_BANKS))
             passes[unit] = bank
             nc.tensor.matmul(
-                out=bank[:].rearrange("p c j -> p (c j)"),
+                out=bank[:].rearrange("p (c i) j -> p c j i", i=RUN),
                 lhsT=identity[:],
-                rhs=raw[unit][1][:, :, CHUNK - PE_COLS :].rearrange("p j c -> p c j"),
+                rhs=raw[unit][1][:, :, CHUNK - PE_COLS :].rearrange("p j (c i) -> p c j i", i=RUN),
                 start=True,
                 stop=True,
             )

@@ -23,7 +23,6 @@ LOAD_COLS = 2 * CHUNK
 TAIL_COLS = P
 TAIL_UNITS = LOAD_COLS // TAIL_COLS
 TAIL_VECTOR = 48
-TAIL_LOAD = 6 * P
 STORE_COLS = CHUNK // 2
 PE_COLS = P
 PE_BANKS = 4
@@ -65,7 +64,7 @@ def tile_quaternionlinear_kernel(tc, x, Wr, Wi, Wj, Wk, br, bi, bj, bk, grad_out
                 for name in ("g", "x"):
                     piece = raw_pool.tile([P, PACK, LOAD_COLS], BF16, name="raw_%s_%d_%d" % (name, half, load_col))
                     last = name == "x" and half == TOKEN_HALVES - 1 and load_col == COLS - LOAD_COLS
-                    cuts = [0, TAIL_LOAD, LOAD_COLS] if last else [0, LOAD_COLS]
+                    cuts = [0, LOAD_COLS]
                     for begin, end in zip(cuts, cuts[1:]):
                         nc.sync.dma_start(
                             out=piece[:, :, begin:end],

from contextlib import ExitStack

import concourse.mybir as mybir
from concourse.masks import make_identity

BF16 = mybir.dt.bfloat16
F32 = mybir.dt.float32
U32 = mybir.dt.uint32
U8 = mybir.dt.uint8
E4M3_X4 = mybir.dt.float8_e4m3fn_x4
E5M2_X4 = mybir.dt.float8_e5m2_x4

P = 128
PACK = 4
K_PASS = P * PACK
TOKENS = 1024
TOKEN_HALVES = TOKENS // K_PASS
CHUNK = 512
CHUNKS = 4
COLS = CHUNKS * CHUNK
M_TILES = CHUNK // P
LOAD_COLS = 2 * CHUNK
TAIL_COLS = P
TAIL_UNITS = LOAD_COLS // TAIL_COLS
TAIL_VECTOR = 48
STORE_COLS = CHUNK // 2
PE_COLS = P
PE_BANKS = 4
RUN = 4

FLOPS = 2 * CHUNK * CHUNK * CHUNKS * TOKENS
BYTES = 2 * TOKENS * COLS * 2 + CHUNK * CHUNK * 4


def tile_quaternionlinear_kernel(tc, x, Wr, Wi, Wj, Wk, br, bi, bj, bk, grad_out, out):
    nc = tc.nc
    sources = {"x": x, "g": grad_out}
    formats = {"x": E4M3_X4, "g": E5M2_X4}

    with ExitStack() as ctx:
        raw_pool = ctx.enter_context(tc.tile_pool(name="raw", bufs=1))
        grouped_pool = ctx.enter_context(tc.tile_pool(name="grouped", bufs=1))
        keep = ctx.enter_context(tc.tile_pool(name="keep", bufs=1))
        result_pool = ctx.enter_context(tc.tile_pool(name="result", bufs=1))
        psum = ctx.enter_context(tc.psum_pool(name="psum", bufs=1))
        ctx.enter_context(tc.manual_schedule())

        codes = {}
        scales = {}
        for name in ("x", "g"):
            codes[name] = keep.tile([P, TOKEN_HALVES, COLS], U32, name="codes_" + name, align_bytes=64)
            scales[name] = keep.tile([P, TOKEN_HALVES, COLS], U8, name="scales_" + name, align_bytes=64)
        tail_codes = keep.tile([P, TAIL_UNITS, TAIL_COLS], U32, name="tail_codes", align_bytes=64)
        tail_scales = keep.tile([P, TAIL_UNITS, TAIL_COLS], U8, name="tail_scales", align_bytes=64)
        identity = keep.tile([P, P], BF16, name="identity")
        make_identity(nc, identity[:])
        acc = [psum.tile([P, CHUNK], F32, name="acc_%d" % m) for m in range(M_TILES)]

        raw = {}
        units = []
        for half in range(TOKEN_HALVES):
            token_rows = slice(half * K_PASS, (half + 1) * K_PASS)
            for load_col in range(0, COLS, LOAD_COLS):
                for name in ("g", "x"):
                    piece = raw_pool.tile([P, PACK, LOAD_COLS], BF16, name="raw_%s_%d_%d" % (name, half, load_col))
                    last = name == "x" and half == TOKEN_HALVES - 1 and load_col == COLS - LOAD_COLS
                    cuts = [0, LOAD_COLS]
                    for begin, end in zip(cuts, cuts[1:]):
                        nc.sync.dma_start(
                            out=piece[:, :, begin:end],
                            in_=sources[name][token_rows, load_col + begin : load_col + end].rearrange(
                                "(p j) w -> p j w", j=PACK
                            ),
                        )
                    if last:
                        for n in range(TAIL_UNITS):
                            m, k = divmod(n, 2)
                            unit = ("tail", half, n, TAIL_COLS)
                            first = k * CHUNK + m * P
                            raw[unit] = [piece[:, :, first : first + TAIL_VECTOR], piece[:, :, first + TAIL_VECTOR : first + TAIL_COLS]]
                            units.append(unit)
                    else:
                        for col in range(load_col, load_col + LOAD_COLS, CHUNK):
                            unit = (name, half, col, CHUNK)
                            first = col - load_col
                            raw[unit] = [piece[:, :, first : first + CHUNK] if col == load_col else None,
                                         piece[:, :, first : first + CHUNK] if col != load_col else None]
                            units.append(unit)

        grouped = {}

        passes = {}

        def tensor_pass(unit):
            n = len(passes)
            bank = psum.tile([P, PE_COLS, PACK], BF16, name="bank_%d" % (n % PE_BANKS))
            passes[unit] = bank
            nc.tensor.matmul(
                out=bank[:].rearrange("p (c i) j -> p c j i", i=RUN),
                lhsT=identity[:],
                rhs=raw[unit][1][:, :, CHUNK - PE_COLS :].rearrange("p j (c i) -> p c j i", i=RUN),
                start=True,
                stop=True,
            )

        def regroup(unit):
            width = unit[3]
            tile = grouped_pool.tile([P, width, PACK], BF16, name="grouped_%s_%d_%d_%d" % unit, align_bytes=64)
            grouped[unit] = tile
            whole = unit[0] != "tail"
            if raw[unit][0] is not None:
                nc.vector.tensor_copy(
                    out=tile[:, : width if whole else TAIL_VECTOR, :].rearrange("p (c i) j -> p c j i", i=RUN),
                    in_=raw[unit][0].rearrange("p j (c i) -> p c j i", i=RUN),
                )
            if raw[unit][1] is not None:
                begin = 0 if whole else TAIL_VECTOR
                end = width - PE_COLS if unit in passes else width
                nc.scalar.copy(
                    out=tile[:, begin:end, :].rearrange("p (c i) j -> p c j i", i=RUN),
                    in_=raw[unit][1][:, :, : end - begin].rearrange("p j (c i) -> p c j i", i=RUN),
                )
                if unit in passes:
                    nc.scalar.copy(out=tile[:, end:, :], in_=passes[unit][:])

        def quantise(unit):
            name, half, col, width = unit
            if name == "tail":
                codes_out = tail_codes[:, col, :].bitcast(E4M3_X4)
                scales_out = tail_scales[:, col, :]
            else:
                codes_out = codes[name][:, half, col : col + width].bitcast(formats[name])
                scales_out = scales[name][:, half, col : col + width]
            nc.vector.quantize_mx(out=codes_out, scales=scales_out, in_=grouped[unit][:].rearrange("p w j -> p (w j)"))

        def multiply(unit):
            name, half, col, width = unit
            for k in range(width // P):
                if name == "tail":
                    m = col // 2
                    chunk = CHUNKS - 2 + col % 2
                    x_codes = tail_codes[:, col, :]
                    x_scales = tail_scales[:, col, :]
                else:
                    m = k
                    chunk = col // CHUNK
                    x_codes = codes["x"][:, half, col + k * P : col + (k + 1) * P]
                    x_scales = scales["x"][:, half, col + k * P : col + (k + 1) * P]
                chunk_cols = slice(chunk * CHUNK, (chunk + 1) * CHUNK)
                nc.tensor.matmul_mx(
                    out=acc[m][:],
                    lhsT=x_codes.bitcast(E4M3_X4),
                    lhsT_scale=x_scales,
                    rhs=codes["g"][:, half, chunk_cols].bitcast(E5M2_X4),
                    rhs_scale=scales["g"][:, half, chunk_cols],
                    start=(half == 0 and chunk == 0),
                    stop=(half == TOKEN_HALVES - 1 and chunk == CHUNKS - 1),
                )

        def finish(unit):
            quantise(unit)
            if unit[0] != "g":
                multiply(unit)

        waiting = []
        for i, unit in enumerate(units):
            regroup(unit)
            if i % 2 == 1 and i + 2 < len(units) - TAIL_UNITS:
                tensor_pass(units[i + 2])
            if unit[0] == "tail" or i % 2 == 1:
                if unit[0] == "tail":
                    finish(waiting.pop(0))
                    waiting.append(unit)
                else:
                    if len(waiting) == 2:
                        finish(waiting.pop(0))
                    finish(waiting.pop(0))
                    waiting.append(unit)
            else:
                waiting.append(unit)
        for unit in waiting:
            finish(unit)

        for m in range(M_TILES):
            for col in range(0, CHUNK, STORE_COLS):
                result = result_pool.tile([P, STORE_COLS], F32, name="result_%d_%d" % (m, col))
                if m < M_TILES - 1:
                    nc.scalar.copy(out=result[:], in_=acc[m][:, col : col + STORE_COLS])
                else:
                    nc.vector.tensor_copy(out=result[:], in_=acc[m][:, col : col + STORE_COLS])
                nc.sync.dma_start(out=out[m * P : (m + 1) * P, col : col + STORE_COLS], in_=result[:])
